import numpy as np
import ml_dtypes


def mxq(x, axis, fmt="e4m3"):
    dtype, down = {"e4m3": (ml_dtypes.float8_e4m3fn, 7), "e5m2": (ml_dtypes.float8_e5m2, 14)}[fmt]
    v = np.moveaxis(np.asarray(x, np.float32).astype(ml_dtypes.bfloat16).astype(np.float64), axis, -1)
    blocks = v.reshape(v.shape[:-1] + (-1, 32))
    amax = np.abs(blocks).max(-1, keepdims=True)
    byte = np.maximum(np.where(amax > 0, np.frexp(amax)[1] - 1 + 127, 0) - down, 1)
    scale = np.exp2(byte - 127.0)
    codes = (blocks / scale).astype(np.float32).astype(dtype).astype(np.float64)
    return np.moveaxis((codes * scale).reshape(v.shape), -1, axis)


WIDE = False


def mx_kscale(k):
    if not WIDE:
        return np.ones(k)
    levels = np.array([10, -10, 5, -5, 0])
    if k % 512:
        return np.exp2(np.random.permutation(np.resize(levels, k // 32))).repeat(32)
    a = np.empty((k // 512, 16))
    for p in range(k // 512):
        a[p, :8] = np.random.permutation(np.resize(levels, 8))
        for g in range(8):
            far = levels[np.abs(levels - a[p, g]) >= 10]
            a[p, g + 8] = far[np.random.randint(len(far))]
    return np.exp2(a.ravel()).repeat(32)


BF16 = ml_dtypes.bfloat16


def bf(x):
    return np.asarray(x, np.float32).astype(BF16)


def f64(x):
    return np.asarray(x).astype(np.float64)


B, C, HH, WW = 1, 2048, 64, 64
N = HH * WW


def setup_inputs():
    s, t = mx_kscale(C), mx_kscale(C)
    return {"x": bf(np.random.standard_normal((B, C, HH, WW)) * s[None, :, None, None]),
            "Wq": bf(np.random.standard_normal((C, C)) * 1.4 / np.sqrt(C) * t[:, None] / s[None, :]),
            "bq": bf(np.random.standard_normal(C) * 0.2 * t),
            "k": bf(np.random.standard_normal((B, N, C)) * 1.4 / t)}


def reference(x, Wq, bq, k):
    xt = f64(x).reshape(B, C, N)
    q = (mxq(xt, 1, "e4m3").transpose(0, 2, 1) @ mxq(f64(Wq), 1, "e4m3").T) + f64(bq)
    scores = mxq(q / np.sqrt(C), 2, "e4m3") @ mxq(f64(k), 2, "e4m3").transpose(0, 2, 1)
    e = np.exp(scores - scores.max(-1, keepdims=True))
    return e / e.sum(-1, keepdims=True)

@@ -1,0 +1,342 @@
+import math
+from contextlib import ExitStack
+
+import concourse.masks as masks
+import concourse.mybir as mybir
+
+F32 = mybir.dt.float32
+BF16 = mybir.dt.bfloat16
+U32 = mybir.dt.uint32
+U8 = mybir.dt.uint8
+FP8X4 = mybir.dt.float8_e4m3fn_x4
+ALU = mybir.AluOpType
+ACT = mybir.ActivationFunctionType
+AXIS = mybir.AxisListType
+
+P = 128
+C = 2048
+TOKENS = 4096
+KEYS = 4096
+PASSES = 4
+BANK = 512
+N_BLOCKS = TOKENS // BANK
+N_UNITS = 4 * N_BLOCKS
+N_W_RUNS = 8
+N_RUNS = 24
+N_TILES = TOKENS // P
+RAW_BUFS = 3
+X_BUFS = 4
+GRP_BUFS = 5
+SCORE_BUFS = 6
+HEAD_X_ON_SCALAR = 192
+LATE_X_ON_SCALAR = 256
+
+FLOPS = 2 * TOKENS * C * C + 2 * TOKENS * KEYS * C
+
+
+def tile_visionattention_pa_l_kernel(tc, x, Wq, bq, k, out):
+    nc = tc.nc
+    inv_sqrt_c = 1.0 / math.sqrt(C)
+    x2 = x.rearrange("b c h w -> (b c) (h w)")
+    k2 = k.rearrange("b m c -> (b m) c")
+    out2 = out.rearrange("b n m -> (b n) m")
+
+    with ExitStack() as ctx:
+        keep = ctx.enter_context(tc.tile_pool(name="keep", bufs=1))
+        rawq = ctx.enter_context(tc.tile_pool(name="rawq", bufs=RAW_BUFS))
+        psum = ctx.enter_context(tc.psum_pool(name="psum", bufs=8))
+
+        ident = keep.tile([P, P], F32, name="ident")
+        masks.make_identity(nc, ident[:])
+
+        ctx.enter_context(tc.manual_schedule())
+
+        bq_raw = keep.tile([P, 4, 4], BF16, name="bq_raw")
+        nc.scalar.dma_start(out=bq_raw[:], in_=bq.rearrange("(a p t) -> p a t", a=4, t=4))
+        warm = keep.tile([P, 1], F32, name="warm")
+        nc.vector.memset(warm[:], 0.0)
+        nc.scalar.activation(out=warm[:], in_=warm[:], func=ACT.Exp)
+        bias = keep.tile([P, 16], F32, name="bias")
+
+        k_codes = []
+        k_planes = []
+        q_codes = []
+        q_planes = []
+        for i in range(8):
+            k_codes.append(keep.tile([P, PASSES, BANK], U32, name="k_codes%d" % i, align_bytes=64))
+            k_planes.append(keep.tile([P, BANK], U8, name="k_planes%d" % i, align_bytes=64))
+            q_planes.append(keep.tile([P, BANK], U8, name="q_planes%d" % i, align_bytes=64))
+        for i in range(N_BLOCKS - RAW_BUFS):
+            q_codes.append(keep.tile([P, PASSES, BANK], U32, name="q_codes%d" % i, align_bytes=64))
+
+        def quantize(grp, codes, planes, g):
+            nc.vector.quantize_mx(
+                out=codes[:, g, :].bitcast(FP8X4),
+                scales=planes[4 * g : P, :],
+                in_=grp[:].rearrange("p n j -> p (n j)"),
+            )
+
+        def mx_bank(stat_codes, stat_planes, cols, mov_codes, mov_planes):
+            acc = psum.tile([P, BANK], F32, name="acc", tag="bank")
+            for g in range(PASSES):
+                nc.tensor.matmul_mx(
+                    out=acc[:],
+                    lhsT=stat_codes[:, g, cols].bitcast(FP8X4),
+                    lhsT_scale=stat_planes[4 * g : P, cols],
+                    rhs=mov_codes[:, g, :].bitcast(FP8X4),
+                    rhs_scale=mov_planes[4 * g : P, :],
+                    start=(g == 0),
+                    stop=(g == PASSES - 1),
+                )
+            return acc
+
+        with tc.tile_pool(name="ph1", bufs=1) as ph1:
+            w_codes = []
+            w_planes = []
+            for i in range(4):
+                w_codes.append(ph1.tile([P, PASSES, BANK], U32, name="w_codes%d" % i, align_bytes=64))
+                w_planes.append(ph1.tile([P, BANK], U8, name="w_planes%d" % i, align_bytes=64))
+
+            raws = {}
+            xraws = {}
+            xgrps = {}
+            x_codes = {}
+            x_planes = {}
+            qbfs = {}
+            qgrps = {}
+            tgrps = {}
+
+            def load_raw(r):
+                raw = rawq.tile([P, 4, 1024], BF16, name="raw", tag="rawq", align_bytes=64)
+                if r < N_W_RUNS:
+                    a, h = divmod(r, 2)
+                    src = Wq[512 * a : 512 * (a + 1), 1024 * h : 1024 * (h + 1)].rearrange("(m t) c -> m t c", t=4)
+                else:
+                    a, h = divmod(r - N_W_RUNS, 2)
+                    src = k2[512 * a : 512 * (a + 1), 1024 * h : 1024 * (h + 1)].rearrange("(a p) c -> p a c", p=P)
+                nc.sync.dma_start(out=raw[:], in_=src)
+                raws[r] = raw
+
+            def load_x(c):
+                b, g = divmod(c, 4)
+                xr = ph1.tile([P, 4, BANK], BF16, name="xr", tag="xr", bufs=X_BUFS, align_bytes=64)
+                src = x2[512 * g : 512 * (g + 1), BANK * b : BANK * (b + 1)].rearrange("(p j) n -> p j n", j=4)
+                nc.sync.dma_start(out=xr[:], in_=src)
+                xraws[c] = xr
+
+            def new_grp():
+                grp = ph1.tile([P, BANK, 4], BF16, name="grp", tag="grp", bufs=GRP_BUFS, align_bytes=64)
+                return grp
+
+            def interleave_x(c, on_scalar):
+                grp = new_grp()
+                xr = xraws[c]
+                cut = BANK - on_scalar
+                nc.vector.tensor_copy(out=grp[:, 0:cut, :], in_=xr[:, :, 0:cut].rearrange("p j n -> p n j"))
+                if on_scalar > 0:
+                    nc.scalar.copy(out=grp[:, cut:BANK, :], in_=xr[:, :, cut:BANK].rearrange("p j n -> p n j"))
+                xgrps[c] = grp
+
+            def quantize_x(c):
+                b, g = divmod(c, 4)
+                if g == 0:
+                    x_codes[b] = ph1.tile([P, PASSES, BANK], U32, name="xc", tag="xc", bufs=2, align_bytes=64)
+                    x_planes[b] = ph1.tile([P, BANK], U8, name="xp", tag="xp", bufs=2, align_bytes=64)
+                quantize(xgrps[c], x_codes[b], x_planes[b], g)
+
+            def transpose_run(r):
+                words = raws[r][:].bitcast(F32)
+                banks = []
+                for gl in range(2):
+                    for ah in range(2):
+                        tp = psum.tile([P, 2, 2, P], F32, name="tp", tag="bank")
+                        for aa in range(2):
+                            for u in range(2):
+                                nc.tensor.transpose(
+                                    tp[:, aa, u, :],
+                                    words[:, 2 * ah + aa, 256 * gl + u : 256 * (gl + 1) : 2],
+                                    ident[:],
+                                )
+                        banks.append(tp)
+                return banks
+
+            def copy_out_run(r, banks):
+                grps = []
+                for gl in range(2):
+                    grp = new_grp()
+                    gw = grp[:].bitcast(F32)
+                    for ah in range(2):
+                        nc.scalar.copy(
+                            out=gw[:, 256 * ah : 256 * (ah + 1), :].rearrange("p (a r) u -> p a r u", a=2),
+                            in_=banks[2 * gl + ah][:].rearrange("p a u r -> p a r u"),
+                        )
+                    grps.append(grp)
+                tgrps[r] = grps
+
+            def quantize_run(r):
+                if r < N_W_RUNS:
+                    a, h = divmod(r, 2)
+                    codes, planes = w_codes[a], w_planes[a]
+                else:
+                    a, h = divmod(r - N_W_RUNS, 2)
+                    codes, planes = k_codes[a], k_planes[a]
+                for gl in range(2):
+                    quantize(tgrps[r][gl], codes, planes, 2 * h + gl)
+
+            def project_half(u, hf):
+                b, a = divmod(u, 4)
+                banks = []
+                for t in (2 * hf, 2 * hf + 1):
+                    banks.append(mx_bank(w_codes[a], w_planes[a], slice(P * t, P * (t + 1)), x_codes[b], x_planes[b]))
+                return banks
+
+            def evacuate_half(u, hf, banks):
+                a = u % 4
+                if hf == 0:
+                    qbfs[u] = ph1.tile([P, 4, BANK], BF16, name="qbf", tag="qbf", bufs=2, align_bytes=64)
+                for i in range(2):
+                    t = 2 * hf + i
+                    nc.scalar.activation(
+                        out=qbfs[u][:, t, :],
+                        in_=banks[i][:],
+                        func=ACT.Identity,
+                        bias=bias[:, 4 * a + t : 4 * a + t + 1],
+                        scale=inv_sqrt_c,
+                    )
+
+            def interleave_q(u):
+                grp = new_grp()
+                nc.vector.tensor_copy(out=grp[:], in_=qbfs[u][:].rearrange("p t n -> p n t"))
+                qgrps[u] = grp
+
+            def quantize_q(u):
+                b, a = divmod(u, 4)
+                if a == 0 and b >= len(q_codes):
+                    q_codes.append(rawq.tile([P, PASSES, BANK], U32, name="q_late", tag="rawq", align_bytes=64))
+                quantize(qgrps[u], q_codes[b], q_planes[b], a)
+
+            items = [("R", 0, 0), ("R", 1, 0), ("R", 2, 0)]
+            r_next = 3
+            for u in range(N_UNITS):
+                for hf in range(2):
+                    items.append(("U", u, hf))
+                    if r_next < N_RUNS and (u < 4 or hf == 1):
+                        items.append(("R", r_next, 0))
+                        r_next += 1
+
+            for r in range(RAW_BUFS):
+                load_raw(r)
+            for c in range(4):
+                load_x(c)
+            nc.vector.tensor_scalar(
+                out=bias[:], in0=bq_raw[:].rearrange("p a t -> p (a t)"), scalar1=inv_sqrt_c, scalar2=None, op0=ALU.mult
+            )
+
+            pending_q = []
+            prev = None
+            head_x_done = False
+            for item in items:
+                kind, n, hf = item
+                x_chunk = None
+                if kind == "U" and not head_x_done:
+                    for c in range(4):
+                        interleave_x(c, HEAD_X_ON_SCALAR)
+                        load_x(c + X_BUFS)
+                        if c > 0:
+                            quantize_x(c - 1)
+                    if prev is not None and prev[0] == "R":
+                        quantize_run(prev[1])
+                        prev = None
+                    quantize_x(3)
+                    head_x_done = True
+                if kind == "R":
+                    banks = transpose_run(n)
+                    if n + RAW_BUFS < N_RUNS:
+                        load_raw(n + RAW_BUFS)
+                else:
+                    banks = project_half(n, hf)
+                if kind == "U" and hf == 0 and n + 4 < N_UNITS:
+                    x_chunk = n + 4
+                    interleave_x(x_chunk, LATE_X_ON_SCALAR if r_done(n) else 0)
+                    if x_chunk + X_BUFS < N_UNITS:
+                        load_x(x_chunk + X_BUFS)
+                if kind == "R":
+                    copy_out_run(n, banks)
+                else:
+                    evacuate_half(n, hf, banks)
+                for u in pending_q:
+                    quantize_q(u)
+                pending_q = []
+                if prev is not None:
+                    if prev[0] == "R":
+                        quantize_run(prev[1])
+                    elif prev[2] == 1:
+                        interleave_q(prev[1])
+                        pending_q.append(prev[1])
+                if x_chunk is not None:
+                    quantize_x(x_chunk)
+                prev = item
+            interleave_q(prev[1])
+            quantize_q(prev[1])
+
+        with tc.tile_pool(name="ph2", bufs=4) as ph2:
+            state = {}
+
+            def soft_exp(s):
+                sc, negmax = state[s]
+                tot = ph2.tile([P, 1], F32, name="tot", tag="tot")
+                nc.scalar.activation(out=sc[:], in_=sc[:], func=ACT.Exp, bias=negmax[:], scale=-1.0, accum_out=tot[:])
+                state[s] = (sc, tot)
+
+            def soft_finish(s, last):
+                sc, tot = state[s]
+                rs = ph2.tile([P, 1], F32, name="rs", tag="rs")
+                nc.vector.reciprocal(out=rs[:], in_=tot[:])
+                rows = slice(P * s, P * (s + 1))
+                if not last:
+                    for h in range(2):
+                        cols = slice(2048 * h, 2048 * (h + 1))
+                        nc.gpsimd.tensor_scalar(
+                            out=sc[:, cols], in0=sc[:, cols], scalar1=rs[:], scalar2=0.0, op0=ALU.mult, op1=ALU.add
+                        )
+                        nc.sync.dma_start(out=out2[rows, cols], in_=sc[:, cols])
+                else:
+                    nc.gpsimd.tensor_scalar(
+                        out=sc[:, 3072:4096], in0=sc[:, 3072:4096], scalar1=rs[:], scalar2=0.0, op0=ALU.mult, op1=ALU.add
+                    )
+                    nc.scalar.activation(out=sc[:, 2048:3072], in_=sc[:, 2048:3072], func=ACT.Copy, scale=rs[:])
+                    for h in range(2):
+                        cols = slice(1024 * h, 1024 * (h + 1))
+                        nc.vector.tensor_scalar(out=sc[:, cols], in0=sc[:, cols], scalar1=rs[:], scalar2=None, op0=ALU.mult)
+                        nc.sync.dma_start(out=out2[rows, cols], in_=sc[:, cols])
+                    nc.sync.dma_start(out=out2[rows, 2048:3072], in_=sc[:, 2048:3072])
+                    nc.sync.dma_start(out=out2[rows, 3072:4096], in_=sc[:, 3072:4096])
+
+            for s in range(N_TILES):
+                b, j = divmod(s, 4)
+                if s > 0:
+                    soft_exp(s - 1)
+                sc = ph2.tile([P, KEYS], F32, name="sc", tag="sc", bufs=SCORE_BUFS)
+                nm = ph2.tile([P, 8], F32, name="nm", tag="nm")
+                for kb in range(8):
+                    acc = mx_bank(q_codes[b], q_planes[b], slice(P * j, P * (j + 1)), k_codes[kb], k_planes[kb])
+                    nc.vector.tensor_scalar(
+                        out=sc[:, BANK * kb : BANK * (kb + 1)],
+                        in0=acc[:],
+                        scalar1=-1.0,
+                        scalar2=None,
+                        op0=ALU.mult,
+                        op1=ALU.min,
+                        accum_out=nm[:, kb : kb + 1],
+                    )
+                    if kb == 4 and s > 0:
+                        soft_finish(s - 1, False)
+                negmax = ph2.tile([P, 1], F32, name="negmax", tag="negmax")
+                nc.vector.tensor_reduce(out=negmax[:], in_=nm[:], axis=AXIS.X, op=ALU.min)
+                state[s] = (sc, negmax)
+            soft_exp(N_TILES - 1)
+            soft_finish(N_TILES - 1, True)
+
+
+def r_done(u):
+    return u >= 17

@@ -30,6 +30,9 @@ GRP_BUFS = 5
 SCORE_BUFS = 6
 HEAD_X_ON_SCALAR = 192
 LATE_X_ON_SCALAR = 256
+FIRST_UNIT_WITHOUT_RUN = 18
+NORM_ON_VECTOR = 2688
+X_CHUNK_AT = {(1, 0): 4, (1, 1): 5, (2, 0): 6, (3, 0): 7}
 
 FLOPS = 2 * TOKENS * C * C + 2 * TOKENS * KEYS * C
 
@@ -76,6 +79,9 @@ def tile_visionattention_pa_l_kernel(tc, x, Wq, bq, k, out):
                 in_=grp[:].rearrange("p n j -> p (n j)"),
             )
 
+        def packed(planes):
+            return [planes[4 * g : P, :] for g in range(PASSES)]
+
         def mx_bank(stat_codes, stat_planes, cols, mov_codes, mov_planes):
             acc = psum.tile([P, BANK], F32, name="acc", tag="bank")
             for g in range(PASSES):
@@ -84,7 +90,7 @@ def tile_visionattention_pa_l_kernel(tc, x, Wq, bq, k, out):
                     lhsT=stat_codes[:, g, cols].bitcast(FP8X4),
                     lhsT_scale=stat_planes[4 * g : P, cols],
                     rhs=mov_codes[:, g, :].bitcast(FP8X4),
-                    rhs_scale=mov_planes[4 * g : P, :],
+                    rhs_scale=mov_planes[g],
                     start=(g == 0),
                     stop=(g == PASSES - 1),
                 )
@@ -141,8 +147,12 @@ def tile_visionattention_pa_l_kernel(tc, x, Wq, bq, k, out):
                 b, g = divmod(c, 4)
                 if g == 0:
                     x_codes[b] = ph1.tile([P, PASSES, BANK], U32, name="xc", tag="xc", bufs=2, align_bytes=64)
-                    x_planes[b] = ph1.tile([P, BANK], U8, name="xp", tag="xp", bufs=2, align_bytes=64)
-                quantize(xgrps[c], x_codes[b], x_planes[b], g)
+                x_planes[c] = ph1.tile([P, BANK], U8, name="xp", tag="xp", bufs=8, align_bytes=64)
+                nc.vector.quantize_mx(
+                    out=x_codes[b][:, g, :].bitcast(FP8X4),
+                    scales=x_planes[c][:],
+                    in_=xgrps[c][:].rearrange("p n j -> p (n j)"),
+                )
 
             def transpose_run(r):
                 words = raws[r][:].bitcast(F32)
@@ -173,29 +183,54 @@ def tile_visionattention_pa_l_kernel(tc, x, Wq, bq, k, out):
                     grps.append(grp)
                 tgrps[r] = grps
 
-            def quantize_run(r):
+            def quantize_run(r, gl):
                 if r < N_W_RUNS:
                     a, h = divmod(r, 2)
                     codes, planes = w_codes[a], w_planes[a]
                 else:
                     a, h = divmod(r - N_W_RUNS, 2)
                     codes, planes = k_codes[a], k_planes[a]
-                for gl in range(2):
-                    quantize(tgrps[r][gl], codes, planes, 2 * h + gl)
+                quantize(tgrps[r][gl], codes, planes, 2 * h + gl)
 
             def project_half(u, hf):
                 b, a = divmod(u, 4)
                 banks = []
                 for t in (2 * hf, 2 * hf + 1):
-                    banks.append(mx_bank(w_codes[a], w_planes[a], slice(P * t, P * (t + 1)), x_codes[b], x_planes[b]))
+                    banks.append(
+                        mx_bank(
+                            w_codes[a],
+                            w_planes[a],
+                            slice(P * t, P * (t + 1)),
+                            x_codes[b],
+                            [x_planes[4 * b + g][:] for g in range(PASSES)],
+                        )
+                    )
                 return banks
 
-            def evacuate_half(u, hf, banks):
+            def project_passes(u, gh, banks):
+                b, a = divmod(u, 4)
+                if gh == 0:
+                    for t in range(4):
+                        banks.append(psum.tile([P, BANK], F32, name="acc", tag="bank"))
+                for g in (2 * gh, 2 * gh + 1):
+                    for t in range(4):
+                        cols = slice(P * t, P * (t + 1))
+                        nc.tensor.matmul_mx(
+                            out=banks[t][:],
+                            lhsT=w_codes[a][:, g, cols].bitcast(FP8X4),
+                            lhsT_scale=w_planes[a][4 * g : P, cols],
+                            rhs=x_codes[b][:, g, :].bitcast(FP8X4),
+                            rhs_scale=x_planes[4 * b + g][:],
+                            start=(g == 0),
+                            stop=(g == PASSES - 1),
+                        )
+
+            def evacuate(u, first, banks):
                 a = u % 4
-                if hf == 0:
+                if first == 0:
                     qbfs[u] = ph1.tile([P, 4, BANK], BF16, name="qbf", tag="qbf", bufs=2, align_bytes=64)
-                for i in range(2):
-                    t = 2 * hf + i
+                for i in range(len(banks)):
+                    t = first + i
                     nc.scalar.activation(
                         out=qbfs[u][:, t, :],
                         in_=banks[i][:],
@@ -215,61 +250,73 @@ def tile_visionattention_pa_l_kernel(tc, x, Wq, bq, k, out):
                     q_codes.append(rawq.tile([P, PASSES, BANK], U32, name="q_late", tag="rawq", align_bytes=64))
                 quantize(qgrps[u], q_codes[b], q_planes[b], a)
 
-            items = [("R", 0, 0), ("R", 1, 0), ("R", 2, 0)]
-            r_next = 3
-            for u in range(N_UNITS):
+            items = [("R", 0, 0), ("R", 1, 0), ("G", 0, 0), ("G", 0, 1), ("R", 2, 0), ("R", 3, 0)]
+            r_next = 4
+            for u in range(1, N_UNITS):
                 for hf in range(2):
-                    items.append(("U", u, hf))
+                    items.append(("G" if u < 4 else "U", u, hf))
                     if r_next < N_RUNS and (u < 4 or hf == 1):
                         items.append(("R", r_next, 0))
                         r_next += 1
 
-            for r in range(RAW_BUFS):
-                load_raw(r)
+            load_raw(0)
+            load_raw(1)
             for c in range(4):
                 load_x(c)
+            load_raw(2)
             nc.vector.tensor_scalar(
                 out=bias[:], in0=bq_raw[:].rearrange("p a t -> p (a t)"), scalar1=inv_sqrt_c, scalar2=None, op0=ALU.mult
             )
 
             pending_q = []
+            open_banks = []
             prev = None
-            head_x_done = False
             for item in items:
                 kind, n, hf = item
-                x_chunk = None
-                if kind == "U" and not head_x_done:
-                    for c in range(4):
-                        interleave_x(c, HEAD_X_ON_SCALAR)
-                        load_x(c + X_BUFS)
-                        if c > 0:
-                            quantize_x(c - 1)
-                    if prev is not None and prev[0] == "R":
-                        quantize_run(prev[1])
-                        prev = None
-                    quantize_x(3)
-                    head_x_done = True
+                if kind == "G" and n == 0:
+                    interleave_x(2 * hf, HEAD_X_ON_SCALAR)
+                    load_x(2 * hf + X_BUFS)
+                    if hf == 0:
+                        quantize_run(prev[1], 0)
+                        quantize_run(prev[1], 1)
+                        quantize_x(0)
+                    interleave_x(2 * hf + 1, HEAD_X_ON_SCALAR)
+                    load_x(2 * hf + 1 + X_BUFS)
+                    if hf == 1:
+                        quantize_x(2)
+                    quantize_x(2 * hf + 1)
+                    prev = None
                 if kind == "R":
                     banks = transpose_run(n)
                     if n + RAW_BUFS < N_RUNS:
                         load_raw(n + RAW_BUFS)
+                elif kind == "G":
+                    if hf == 0:
+                        open_banks = []
+                    project_passes(n, hf, open_banks)
+                    banks = open_banks
                 else:
                     banks = project_half(n, hf)
-                if kind == "U" and hf == 0 and n + 4 < N_UNITS:
-                    x_chunk = n + 4
-                    interleave_x(x_chunk, LATE_X_ON_SCALAR if r_done(n) else 0)
+                x_chunk = X_CHUNK_AT.get((n, hf)) if kind == "G" else (n + 4 if kind == "U" and hf == 0 else None)
+                if x_chunk is not None and x_chunk >= N_UNITS:
+                    x_chunk = None
+                if x_chunk is not None:
+                    interleave_x(x_chunk, LATE_X_ON_SCALAR if n >= FIRST_UNIT_WITHOUT_RUN else 0)
                     if x_chunk + X_BUFS < N_UNITS:
                         load_x(x_chunk + X_BUFS)
                 if kind == "R":
                     copy_out_run(n, banks)
-                else:
-                    evacuate_half(n, hf, banks)
+                elif kind == "U":
+                    evacuate(n, 2 * hf, banks)
+                elif hf == 1:
+                    evacuate(n, 0, banks)
                 for u in pending_q:
                     quantize_q(u)
                 pending_q = []
                 if prev is not None:
                     if prev[0] == "R":
-                        quantize_run(prev[1])
+                        quantize_run(prev[1], 0)
+                        quantize_run(prev[1], 1)
                     elif prev[2] == 1:
                         interleave_q(prev[1])
                         pending_q.append(prev[1])
@@ -288,29 +335,20 @@ def tile_visionattention_pa_l_kernel(tc, x, Wq, bq, k, out):
                 nc.scalar.activation(out=sc[:], in_=sc[:], func=ACT.Exp, bias=negmax[:], scale=-1.0, accum_out=tot[:])
                 state[s] = (sc, tot)
 
-            def soft_finish(s, last):
+            def soft_finish(s):
                 sc, tot = state[s]
                 rs = ph2.tile([P, 1], F32, name="rs", tag="rs")
                 nc.vector.reciprocal(out=rs[:], in_=tot[:])
                 rows = slice(P * s, P * (s + 1))
-                if not last:
-                    for h in range(2):
-                        cols = slice(2048 * h, 2048 * (h + 1))
-                        nc.gpsimd.tensor_scalar(
-                            out=sc[:, cols], in0=sc[:, cols], scalar1=rs[:], scalar2=0.0, op0=ALU.mult, op1=ALU.add
-                        )
-                        nc.sync.dma_start(out=out2[rows, cols], in_=sc[:, cols])
-                else:
-                    nc.gpsimd.tensor_scalar(
-                        out=sc[:, 3072:4096], in0=sc[:, 3072:4096], scalar1=rs[:], scalar2=0.0, op0=ALU.mult, op1=ALU.add
-                    )
-                    nc.scalar.activation(out=sc[:, 2048:3072], in_=sc[:, 2048:3072], func=ACT.Copy, scale=rs[:])
-                    for h in range(2):
-                        cols = slice(1024 * h, 1024 * (h + 1))
-                        nc.vector.tensor_scalar(out=sc[:, cols], in0=sc[:, cols], scalar1=rs[:], scalar2=None, op0=ALU.mult)
-                        nc.sync.dma_start(out=out2[rows, cols], in_=sc[:, cols])
-                    nc.sync.dma_start(out=out2[rows, 2048:3072], in_=sc[:, 2048:3072])
-                    nc.sync.dma_start(out=out2[rows, 3072:4096], in_=sc[:, 3072:4096])
+                half = NORM_ON_VECTOR // 2
+                nc.scalar.activation(
+                    out=sc[:, NORM_ON_VECTOR:KEYS], in_=sc[:, NORM_ON_VECTOR:KEYS], func=ACT.Copy, scale=rs[:]
+                )
+                for h in range(2):
+                    cols = slice(half * h, half * (h + 1))
+                    nc.vector.tensor_scalar(out=sc[:, cols], in0=sc[:, cols], scalar1=rs[:], scalar2=None, op0=ALU.mult)
+                    nc.sync.dma_start(out=out2[rows, cols], in_=sc[:, cols])
+                nc.sync.dma_start(out=out2[rows, NORM_ON_VECTOR:KEYS], in_=sc[:, NORM_ON_VECTOR:KEYS])
 
             for s in range(N_TILES):
                 b, j = divmod(s, 4)
@@ -319,7 +357,7 @@ def tile_visionattention_pa_l_kernel(tc, x, Wq, bq, k, out):
                 sc = ph2.tile([P, KEYS], F32, name="sc", tag="sc", bufs=SCORE_BUFS)
                 nm = ph2.tile([P, 8], F32, name="nm", tag="nm")
                 for kb in range(8):
-                    acc = mx_bank(q_codes[b], q_planes[b], slice(P * j, P * (j + 1)), k_codes[kb], k_planes[kb])
+                    acc = mx_bank(q_codes[b], q_planes[b], slice(P * j, P * (j + 1)), k_codes[kb], packed(k_planes[kb]))
                     nc.vector.tensor_scalar(
                         out=sc[:, BANK * kb : BANK * (kb + 1)],
                         in0=acc[:],
@@ -330,13 +368,9 @@ def tile_visionattention_pa_l_kernel(tc, x, Wq, bq, k, out):
                         accum_out=nm[:, kb : kb + 1],
                     )
                     if kb == 4 and s > 0:
-                        soft_finish(s - 1, False)
+                        soft_finish(s - 1)
                 negmax = ph2.tile([P, 1], F32, name="negmax", tag="negmax")
                 nc.vector.tensor_reduce(out=negmax[:], in_=nm[:], axis=AXIS.X, op=ALU.min)
                 state[s] = (sc, negmax)
             soft_exp(N_TILES - 1)
-            soft_finish(N_TILES - 1, True)
-
-
-def r_done(u):
-    return u >= 17
+            soft_finish(N_TILES - 1)

@@ -30,9 +30,8 @@ GRP_BUFS = 5
 SCORE_BUFS = 6
 HEAD_X_ON_SCALAR = 192
 LATE_X_ON_SCALAR = 256
-FIRST_UNIT_WITHOUT_RUN = 18
-NORM_ON_VECTOR = 2688
-X_CHUNK_AT = {(1, 0): 4, (1, 1): 5, (2, 0): 6, (3, 0): 7}
+FIRST_UNIT_WITHOUT_RUN = 17
+EXP_PIECES = 4
 
 FLOPS = 2 * TOKENS * C * C + 2 * TOKENS * KEYS * C
 
@@ -79,9 +78,6 @@ def tile_visionattention_pa_l_kernel(tc, x, Wq, bq, k, out):
                 in_=grp[:].rearrange("p n j -> p (n j)"),
             )
 
-        def packed(planes):
-            return [planes[4 * g : P, :] for g in range(PASSES)]
-
         def mx_bank(stat_codes, stat_planes, cols, mov_codes, mov_planes):
             acc = psum.tile([P, BANK], F32, name="acc", tag="bank")
             for g in range(PASSES):
@@ -90,7 +86,7 @@ def tile_visionattention_pa_l_kernel(tc, x, Wq, bq, k, out):
                     lhsT=stat_codes[:, g, cols].bitcast(FP8X4),
                     lhsT_scale=stat_planes[4 * g : P, cols],
                     rhs=mov_codes[:, g, :].bitcast(FP8X4),
-                    rhs_scale=mov_planes[g],
+                    rhs_scale=mov_planes[4 * g : P, :],
                     start=(g == 0),
                     stop=(g == PASSES - 1),
                 )
@@ -147,12 +143,8 @@ def tile_visionattention_pa_l_kernel(tc, x, Wq, bq, k, out):
                 b, g = divmod(c, 4)
                 if g == 0:
                     x_codes[b] = ph1.tile([P, PASSES, BANK], U32, name="xc", tag="xc", bufs=2, align_bytes=64)
-                x_planes[c] = ph1.tile([P, BANK], U8, name="xp", tag="xp", bufs=8, align_bytes=64)
-                nc.vector.quantize_mx(
-                    out=x_codes[b][:, g, :].bitcast(FP8X4),
-                    scales=x_planes[c][:],
-                    in_=xgrps[c][:].rearrange("p n j -> p (n j)"),
-                )
+                    x_planes[b] = ph1.tile([P, BANK], U8, name="xp", tag="xp", bufs=2, align_bytes=64)
+                quantize(xgrps[c], x_codes[b], x_planes[b], g)
 
             def transpose_run(r):
                 words = raws[r][:].bitcast(F32)
@@ -183,54 +175,29 @@ def tile_visionattention_pa_l_kernel(tc, x, Wq, bq, k, out):
                     grps.append(grp)
                 tgrps[r] = grps
 
-            def quantize_run(r, gl):
+            def quantize_run(r):
                 if r < N_W_RUNS:
                     a, h = divmod(r, 2)
                     codes, planes = w_codes[a], w_planes[a]
                 else:
                     a, h = divmod(r - N_W_RUNS, 2)
                     codes, planes = k_codes[a], k_planes[a]
-                quantize(tgrps[r][gl], codes, planes, 2 * h + gl)
+                for gl in range(2):
+                    quantize(tgrps[r][gl], codes, planes, 2 * h + gl)
 
             def project_half(u, hf):
                 b, a = divmod(u, 4)
                 banks = []
                 for t in (2 * hf, 2 * hf + 1):
-                    banks.append(
-                        mx_bank(
-                            w_codes[a],
-                            w_planes[a],
-                            slice(P * t, P * (t + 1)),
-                            x_codes[b],
-                            [x_planes[4 * b + g][:] for g in range(PASSES)],
-                        )
-                    )
+                    banks.append(mx_bank(w_codes[a], w_planes[a], slice(P * t, P * (t + 1)), x_codes[b], x_planes[b]))
                 return banks
 
-            def project_passes(u, gh, banks):
-                b, a = divmod(u, 4)
-                if gh == 0:
-                    for t in range(4):
-                        banks.append(psum.tile([P, BANK], F32, name="acc", tag="bank"))
-                for g in (2 * gh, 2 * gh + 1):
-                    for t in range(4):
-                        cols = slice(P * t, P * (t + 1))
-                        nc.tensor.matmul_mx(
-                            out=banks[t][:],
-                            lhsT=w_codes[a][:, g, cols].bitcast(FP8X4),
-                            lhsT_scale=w_planes[a][4 * g : P, cols],
-                            rhs=x_codes[b][:, g, :].bitcast(FP8X4),
-                            rhs_scale=x_planes[4 * b + g][:],
-                            start=(g == 0),
-                            stop=(g == PASSES - 1),
-                        )
-
-            def evacuate(u, first, banks):
+            def evacuate_half(u, hf, banks):
                 a = u % 4
-                if first == 0:
+                if hf == 0:
                     qbfs[u] = ph1.tile([P, 4, BANK], BF16, name="qbf", tag="qbf", bufs=2, align_bytes=64)
-                for i in range(len(banks)):
-                    t = first + i
+                for i in range(2):
+                    t = 2 * hf + i
                     nc.scalar.activation(
                         out=qbfs[u][:, t, :],
                         in_=banks[i][:],
@@ -250,73 +217,61 @@ def tile_visionattention_pa_l_kernel(tc, x, Wq, bq, k, out):
                     q_codes.append(rawq.tile([P, PASSES, BANK], U32, name="q_late", tag="rawq", align_bytes=64))
                 quantize(qgrps[u], q_codes[b], q_planes[b], a)
 
-            items = [("R", 0, 0), ("R", 1, 0), ("G", 0, 0), ("G", 0, 1), ("R", 2, 0), ("R", 3, 0)]
-            r_next = 4
-            for u in range(1, N_UNITS):
+            items = [("R", 0, 0), ("R", 1, 0), ("R", 2, 0)]
+            r_next = 3
+            for u in range(N_UNITS):
                 for hf in range(2):
-                    items.append(("G" if u < 4 else "U", u, hf))
+                    items.append(("U", u, hf))
                     if r_next < N_RUNS and (u < 4 or hf == 1):
                         items.append(("R", r_next, 0))
                         r_next += 1
 
-            load_raw(0)
-            load_raw(1)
+            for r in range(RAW_BUFS):
+                load_raw(r)
             for c in range(4):
                 load_x(c)
-            load_raw(2)
             nc.vector.tensor_scalar(
                 out=bias[:], in0=bq_raw[:].rearrange("p a t -> p (a t)"), scalar1=inv_sqrt_c, scalar2=None, op0=ALU.mult
             )
 
             pending_q = []
-            open_banks = []
             prev = None
+            head_x_done = False
             for item in items:
                 kind, n, hf = item
-                if kind == "G" and n == 0:
-                    interleave_x(2 * hf, HEAD_X_ON_SCALAR)
-                    load_x(2 * hf + X_BUFS)
-                    if hf == 0:
-                        quantize_run(prev[1], 0)
-                        quantize_run(prev[1], 1)
-                        quantize_x(0)
-                    interleave_x(2 * hf + 1, HEAD_X_ON_SCALAR)
-                    load_x(2 * hf + 1 + X_BUFS)
-                    if hf == 1:
-                        quantize_x(2)
-                    quantize_x(2 * hf + 1)
-                    prev = None
+                x_chunk = None
+                if kind == "U" and not head_x_done:
+                    for c in range(4):
+                        interleave_x(c, HEAD_X_ON_SCALAR)
+                        load_x(c + X_BUFS)
+                        if c > 0:
+                            quantize_x(c - 1)
+                    if prev is not None and prev[0] == "R":
+                        quantize_run(prev[1])
+                        prev = None
+                    quantize_x(3)
+                    head_x_done = True
                 if kind == "R":
                     banks = transpose_run(n)
                     if n + RAW_BUFS < N_RUNS:
                         load_raw(n + RAW_BUFS)
-                elif kind == "G":
-                    if hf == 0:
-                        open_banks = []
-                    project_passes(n, hf, open_banks)
-                    banks = open_banks
                 else:
                     banks = project_half(n, hf)
-                x_chunk = X_CHUNK_AT.get((n, hf)) if kind == "G" else (n + 4 if kind == "U" and hf == 0 else None)
-                if x_chunk is not None and x_chunk >= N_UNITS:
-                    x_chunk = None
-                if x_chunk is not None:
+                if kind == "U" and hf == 0 and n + 4 < N_UNITS:
+                    x_chunk = n + 4
                     interleave_x(x_chunk, LATE_X_ON_SCALAR if n >= FIRST_UNIT_WITHOUT_RUN else 0)
                     if x_chunk + X_BUFS < N_UNITS:
                         load_x(x_chunk + X_BUFS)
                 if kind == "R":
                     copy_out_run(n, banks)
-                elif kind == "U":
-                    evacuate(n, 2 * hf, banks)
-                elif hf == 1:
-                    evacuate(n, 0, banks)
+                else:
+                    evacuate_half(n, hf, banks)
                 for u in pending_q:
                     quantize_q(u)
                 pending_q = []
                 if prev is not None:
                     if prev[0] == "R":
-                        quantize_run(prev[1], 0)
-                        quantize_run(prev[1], 1)
+                        quantize_run(prev[1])
                     elif prev[2] == 1:
                         interleave_q(prev[1])
                         pending_q.append(prev[1])
@@ -329,48 +284,74 @@ def tile_visionattention_pa_l_kernel(tc, x, Wq, bq, k, out):
         with tc.tile_pool(name="ph2", bufs=4) as ph2:
             state = {}
 
-            def soft_exp(s):
-                sc, negmax = state[s]
-                tot = ph2.tile([P, 1], F32, name="tot", tag="tot")
-                nc.scalar.activation(out=sc[:], in_=sc[:], func=ACT.Exp, bias=negmax[:], scale=-1.0, accum_out=tot[:])
-                state[s] = (sc, tot)
-
-            def soft_finish(s):
-                sc, tot = state[s]
-                rs = ph2.tile([P, 1], F32, name="rs", tag="rs")
-                nc.vector.reciprocal(out=rs[:], in_=tot[:])
-                rows = slice(P * s, P * (s + 1))
-                half = NORM_ON_VECTOR // 2
+            def soft_exp(s, e):
+                sc, negmax, tot = state[s]
+                cols = slice(1024 * e, 1024 * (e + 1))
                 nc.scalar.activation(
-                    out=sc[:, NORM_ON_VECTOR:KEYS], in_=sc[:, NORM_ON_VECTOR:KEYS], func=ACT.Copy, scale=rs[:]
+                    out=sc[:, cols], in_=sc[:, cols], func=ACT.Exp, bias=negmax[:], scale=-1.0, accum_out=tot[:, e : e + 1]
                 )
-                for h in range(2):
-                    cols = slice(half * h, half * (h + 1))
-                    nc.vector.tensor_scalar(out=sc[:, cols], in0=sc[:, cols], scalar1=rs[:], scalar2=None, op0=ALU.mult)
-                    nc.sync.dma_start(out=out2[rows, cols], in_=sc[:, cols])
-                nc.sync.dma_start(out=out2[rows, NORM_ON_VECTOR:KEYS], in_=sc[:, NORM_ON_VECTOR:KEYS])
+
+            def soft_finish(s, last):
+                sc, negmax, tot = state[s]
+                tsum = ph2.tile([P, 1], F32, name="tsum", tag="tsum")
+                nc.vector.tensor_reduce(out=tsum[:], in_=tot[:], axis=AXIS.X, op=ALU.add)
+                rs = ph2.tile([P, 1], F32, name="rs", tag="rs")
+                nc.vector.reciprocal(out=rs[:], in_=tsum[:])
+                rows = slice(P * s, P * (s + 1))
+                if not last:
+                    for h in range(2):
+                        cols = slice(2048 * h, 2048 * (h + 1))
+                        nc.gpsimd.tensor_scalar(
+                            out=sc[:, cols], in0=sc[:, cols], scalar1=rs[:], scalar2=0.0, op0=ALU.mult, op1=ALU.add
+                        )
+                        nc.sync.dma_start(out=out2[rows, cols], in_=sc[:, cols])
+                else:
+                    nc.gpsimd.tensor_scalar(
+                        out=sc[:, 3072:4096], in0=sc[:, 3072:4096], scalar1=rs[:], scalar2=0.0, op0=ALU.mult, op1=ALU.add
+                    )
+                    nc.scalar.activation(out=sc[:, 2048:3072], in_=sc[:, 2048:3072], func=ACT.Copy, scale=rs[:])
+                    for h in range(2):
+                        cols = slice(1024 * h, 1024 * (h + 1))
+                        nc.vector.tensor_scalar(out=sc[:, cols], in0=sc[:, cols], scalar1=rs[:], scalar2=None, op0=ALU.mult)
+                        nc.sync.dma_start(out=out2[rows, cols], in_=sc[:, cols])
+                    nc.sync.dma_start(out=out2[rows, 2048:3072], in_=sc[:, 2048:3072])
+                    nc.sync.dma_start(out=out2[rows, 3072:4096], in_=sc[:, 3072:4096])
 
             for s in range(N_TILES):
                 b, j = divmod(s, 4)
-                if s > 0:
-                    soft_exp(s - 1)
                 sc = ph2.tile([P, KEYS], F32, name="sc", tag="sc", bufs=SCORE_BUFS)
                 nm = ph2.tile([P, 8], F32, name="nm", tag="nm")
                 for kb in range(8):
-                    acc = mx_bank(q_codes[b], q_planes[b], slice(P * j, P * (j + 1)), k_codes[kb], packed(k_planes[kb]))
-                    nc.vector.tensor_scalar(
-                        out=sc[:, BANK * kb : BANK * (kb + 1)],
-                        in0=acc[:],
-                        scalar1=-1.0,
-                        scalar2=None,
-                        op0=ALU.mult,
-                        op1=ALU.min,
-                        accum_out=nm[:, kb : kb + 1],
-                    )
-                    if kb == 4 and s > 0:
-                        soft_finish(s - 1)
+                    cols = slice(BANK * kb, BANK * (kb + 1))
+                    if s > 0 and kb % 2 == 0:
+                        soft_exp(s - 1, kb // 2)
+                    acc = mx_bank(q_codes[b], q_planes[b], slice(P * j, P * (j + 1)), k_codes[kb], k_planes[kb])
+                    if kb % 2 == 0:
+                        nc.scalar.activation(out=sc[:, cols], in_=acc[:], func=ACT.Copy, scale=-1.0)
+                    else:
+                        if kb == 7:
+                            if s > 0:
+                                soft_finish(s - 1, False)
+                            nc.vector.tensor_reduce(
+                                out=nm[:, 6:7], in_=sc[:, BANK * 6 : BANK * 7], axis=AXIS.X, op=ALU.min
+                            )
+                        nc.vector.tensor_scalar(
+                            out=sc[:, cols],
+                            in0=acc[:],
+                            scalar1=-1.0,
+                            scalar2=None,
+                            op0=ALU.mult,
+                            op1=ALU.min,
+                            accum_out=nm[:, kb : kb + 1],
+                        )
+                        if kb < 7:
+                            nc.vector.tensor_reduce(
+                                out=nm[:, kb - 1 : kb], in_=sc[:, BANK * (kb - 1) : BANK * kb], axis=AXIS.X, op=ALU.min
+                            )
                 negmax = ph2.tile([P, 1], F32, name="negmax", tag="negmax")
                 nc.vector.tensor_reduce(out=negmax[:], in_=nm[:], axis=AXIS.X, op=ALU.min)
-                state[s] = (sc, negmax)
-            soft_exp(N_TILES - 1)
-            soft_finish(N_TILES - 1)
+                tot = ph2.tile([P, EXP_PIECES], F32, name="tot", tag="tot")
+                state[s] = (sc, negmax, tot)
+            for e in range(EXP_PIECES):
+                soft_exp(N_TILES - 1, e)
+            soft_finish(N_TILES - 1, True)

@@ -17,21 +17,35 @@ P = 128
 C = 2048
 TOKENS = 4096
 KEYS = 4096
-PASSES = 4
+PACK = 4
+PASSES = C // (P * PACK)
 BANK = 512
-N_BLOCKS = TOKENS // BANK
-N_UNITS = 4 * N_BLOCKS
-N_W_RUNS = 8
-N_RUNS = 24
-N_TILES = TOKENS // P
-RAW_BUFS = 3
-X_BUFS = 4
-GRP_BUFS = 5
-SCORE_BUFS = 6
-HEAD_X_ON_SCALAR = 192
-LATE_X_ON_SCALAR = 256
+PSUM_BANKS = 8
+ROW_GROUPS = BANK // P
+PAIRS = P * PACK // 2
+
+BLOCKS = TOKENS // BANK
+UNITS = BLOCKS * (C // BANK)
+TILES = TOKENS // P
+KEY_BANKS = KEYS // BANK
+
+PIECE = 1024
+W_RUNS = (C // BANK) * (C // PIECE)
+RUNS = W_RUNS + (KEYS // BANK) * (C // PIECE)
+UNITS_WITH_TWO_RUNS = 4
 FIRST_UNIT_WITHOUT_RUN = 17
-EXP_PIECES = 4
+
+PIECE_BUFS = 3
+X_BUFS = 4
+GROUPED_BUFS = 5
+SCORE_BUFS = 6
+NEXT_AND_NOW = 2
+STAT_BUFS = 4
+
+X_ON_SCALAR_BLOCK_0 = 192
+X_ON_SCALAR_LATE = 256
+
+FINISH_AFTER_BANK = 4
 
 FLOPS = 2 * TOKENS * C * C + 2 * TOKENS * KEYS * C
 
@@ -45,48 +59,47 @@ def tile_visionattention_pa_l_kernel(tc, x, Wq, bq, k, out):
 
     with ExitStack() as ctx:
         keep = ctx.enter_context(tc.tile_pool(name="keep", bufs=1))
-        rawq = ctx.enter_context(tc.tile_pool(name="rawq", bufs=RAW_BUFS))
-        psum = ctx.enter_context(tc.psum_pool(name="psum", bufs=8))
+        rawq = ctx.enter_context(tc.tile_pool(name="rawq", bufs=PIECE_BUFS))
+        psum = ctx.enter_context(tc.psum_pool(name="psum", bufs=PSUM_BANKS))
 
         ident = keep.tile([P, P], F32, name="ident")
         masks.make_identity(nc, ident[:])
 
         ctx.enter_context(tc.manual_schedule())
 
-        bq_raw = keep.tile([P, 4, 4], BF16, name="bq_raw")
-        nc.scalar.dma_start(out=bq_raw[:], in_=bq.rearrange("(a p t) -> p a t", a=4, t=4))
+        bq_raw = keep.tile([P, PASSES, PACK], BF16, name="bq_raw")
         warm = keep.tile([P, 1], F32, name="warm")
         nc.vector.memset(warm[:], 0.0)
         nc.scalar.activation(out=warm[:], in_=warm[:], func=ACT.Exp)
-        bias = keep.tile([P, 16], F32, name="bias")
+        bias = keep.tile([P, PASSES * PACK], F32, name="bias")
 
         k_codes = []
-        k_planes = []
+        k_scales = []
         q_codes = []
-        q_planes = []
-        for i in range(8):
-            k_codes.append(keep.tile([P, PASSES, BANK], U32, name="k_codes%d" % i, align_bytes=64))
-            k_planes.append(keep.tile([P, BANK], U8, name="k_planes%d" % i, align_bytes=64))
-            q_planes.append(keep.tile([P, BANK], U8, name="q_planes%d" % i, align_bytes=64))
-        for i in range(N_BLOCKS - RAW_BUFS):
-            q_codes.append(keep.tile([P, PASSES, BANK], U32, name="q_codes%d" % i, align_bytes=64))
+        q_scales = []
+        for i in range(KEY_BANKS):
+            k_codes.append(keep.tile([P, PASSES, BANK], U32, name="k_codes%d" % i, align_bytes=256))
+            k_scales.append(keep.tile([P, BANK], U8, name="k_planes%d" % i, align_bytes=64))
+            q_scales.append(keep.tile([P, BANK], U8, name="q_planes%d" % i, align_bytes=64))
+        for i in range(BLOCKS - PIECE_BUFS):
+            q_codes.append(keep.tile([P, PASSES, BANK], U32, name="q_codes%d" % i, align_bytes=256))
 
-        def quantize(grp, codes, planes, g):
+        def quantize(grouped, codes, scales, g):
             nc.vector.quantize_mx(
                 out=codes[:, g, :].bitcast(FP8X4),
-                scales=planes[4 * g : P, :],
-                in_=grp[:].rearrange("p n j -> p (n j)"),
+                scales=scales[4 * g : P, :],
+                in_=grouped[:].rearrange("p n j -> p (n j)"),
             )
 
-        def mx_bank(stat_codes, stat_planes, cols, mov_codes, mov_planes):
+        def mx_bank(stat_codes, stat_scales, cols, mov_codes, mov_scales):
             acc = psum.tile([P, BANK], F32, name="acc", tag="bank")
             for g in range(PASSES):
                 nc.tensor.matmul_mx(
                     out=acc[:],
                     lhsT=stat_codes[:, g, cols].bitcast(FP8X4),
-                    lhsT_scale=stat_planes[4 * g : P, cols],
+                    lhsT_scale=stat_scales[4 * g : P, cols],
                     rhs=mov_codes[:, g, :].bitcast(FP8X4),
-                    rhs_scale=mov_planes[4 * g : P, :],
+                    rhs_scale=mov_scales[4 * g : P, :],
                     start=(g == 0),
                     stop=(g == PASSES - 1),
                 )
@@ -94,264 +107,261 @@ def tile_visionattention_pa_l_kernel(tc, x, Wq, bq, k, out):
 
         with tc.tile_pool(name="ph1", bufs=1) as ph1:
             w_codes = []
-            w_planes = []
-            for i in range(4):
-                w_codes.append(ph1.tile([P, PASSES, BANK], U32, name="w_codes%d" % i, align_bytes=64))
-                w_planes.append(ph1.tile([P, BANK], U8, name="w_planes%d" % i, align_bytes=64))
+            w_scales = []
+            for i in range(PASSES):
+                w_codes.append(ph1.tile([P, PASSES, BANK], U32, name="w_codes%d" % i, align_bytes=256))
+                w_scales.append(ph1.tile([P, BANK], U8, name="w_planes%d" % i, align_bytes=64))
 
-            raws = {}
-            xraws = {}
-            xgrps = {}
+            pieces = {}
+            run_grouped = {}
+            x_loaded = {}
+            x_grouped = {}
             x_codes = {}
-            x_planes = {}
-            qbfs = {}
-            qgrps = {}
-            tgrps = {}
+            x_scales = {}
+            q_bf16 = {}
+            q_grouped = {}
 
-            def load_raw(r):
-                raw = rawq.tile([P, 4, 1024], BF16, name="raw", tag="rawq", align_bytes=64)
-                if r < N_W_RUNS:
+            def load_piece(r):
+                piece = rawq.tile([P, ROW_GROUPS, PIECE], BF16, name="raw", tag="rawq", align_bytes=256)
+                if r < W_RUNS:
                     a, h = divmod(r, 2)
-                    src = Wq[512 * a : 512 * (a + 1), 1024 * h : 1024 * (h + 1)].rearrange("(m t) c -> m t c", t=4)
+                    source = Wq[BANK * a : BANK * (a + 1), PIECE * h : PIECE * (h + 1)].rearrange(
+                        "(m t) c -> m t c", t=ROW_GROUPS
+                    )
                 else:
-                    a, h = divmod(r - N_W_RUNS, 2)
-                    src = k2[512 * a : 512 * (a + 1), 1024 * h : 1024 * (h + 1)].rearrange("(a p) c -> p a c", p=P)
-                nc.sync.dma_start(out=raw[:], in_=src)
-                raws[r] = raw
+                    a, h = divmod(r - W_RUNS, 2)
+                    source = k2[BANK * a : BANK * (a + 1), PIECE * h : PIECE * (h + 1)].rearrange("(t p) c -> p t c", p=P)
+                nc.sync.dma_start(out=piece[:], in_=source)
+                pieces[r] = piece
 
             def load_x(c):
-                b, g = divmod(c, 4)
-                xr = ph1.tile([P, 4, BANK], BF16, name="xr", tag="xr", bufs=X_BUFS, align_bytes=64)
-                src = x2[512 * g : 512 * (g + 1), BANK * b : BANK * (b + 1)].rearrange("(p j) n -> p j n", j=4)
-                nc.sync.dma_start(out=xr[:], in_=src)
-                xraws[c] = xr
+                b, g = divmod(c, PASSES)
+                loaded = ph1.tile([P, PACK, BANK], BF16, name="xr", tag="xr", bufs=X_BUFS, align_bytes=64)
+                source = x2[BANK * g : BANK * (g + 1), BANK * b : BANK * (b + 1)].rearrange("(p j) n -> p j n", j=PACK)
+                nc.sync.dma_start(out=loaded[:], in_=source)
+                x_loaded[c] = loaded
 
-            def new_grp():
-                grp = ph1.tile([P, BANK, 4], BF16, name="grp", tag="grp", bufs=GRP_BUFS, align_bytes=64)
-                return grp
+            def new_grouped():
+                grouped = ph1.tile([P, BANK, PACK], BF16, name="grp", tag="grp", bufs=GROUPED_BUFS, align_bytes=64)
+                return grouped
 
             def interleave_x(c, on_scalar):
-                grp = new_grp()
-                xr = xraws[c]
+                grouped = new_grouped()
+                loaded = x_loaded[c]
                 cut = BANK - on_scalar
-                nc.vector.tensor_copy(out=grp[:, 0:cut, :], in_=xr[:, :, 0:cut].rearrange("p j n -> p n j"))
+                nc.vector.tensor_copy(out=grouped[:, 0:cut, :], in_=loaded[:, :, 0:cut].rearrange("p j n -> p n j"))
                 if on_scalar > 0:
-                    nc.scalar.copy(out=grp[:, cut:BANK, :], in_=xr[:, :, cut:BANK].rearrange("p j n -> p n j"))
-                xgrps[c] = grp
+                    nc.scalar.copy(out=grouped[:, cut:BANK, :], in_=loaded[:, :, cut:BANK].rearrange("p j n -> p n j"))
+                x_grouped[c] = grouped
 
             def quantize_x(c):
-                b, g = divmod(c, 4)
+                b, g = divmod(c, PASSES)
                 if g == 0:
-                    x_codes[b] = ph1.tile([P, PASSES, BANK], U32, name="xc", tag="xc", bufs=2, align_bytes=64)
-                    x_planes[b] = ph1.tile([P, BANK], U8, name="xp", tag="xp", bufs=2, align_bytes=64)
-                quantize(xgrps[c], x_codes[b], x_planes[b], g)
+                    x_codes[b] = ph1.tile([P, PASSES, BANK], U32, name="xc", tag="xc", bufs=NEXT_AND_NOW, align_bytes=256)
+                    x_scales[b] = ph1.tile([P, BANK], U8, name="xp", tag="xp", bufs=NEXT_AND_NOW, align_bytes=64)
+                quantize(x_grouped[c], x_codes[b], x_scales[b], g)
 
             def transpose_run(r):
-                words = raws[r][:].bitcast(F32)
+                pairs = pieces[r][:].bitcast(F32)
                 banks = []
                 for gl in range(2):
-                    for ah in range(2):
-                        tp = psum.tile([P, 2, 2, P], F32, name="tp", tag="bank")
-                        for aa in range(2):
+                    for th in range(2):
+                        turned = psum.tile([P, 2, 2, P], F32, name="tp", tag="bank")
+                        for tl in range(2):
                             for u in range(2):
                                 nc.tensor.transpose(
-                                    tp[:, aa, u, :],
-                                    words[:, 2 * ah + aa, 256 * gl + u : 256 * (gl + 1) : 2],
+                                    turned[:, tl, u, :],
+                                    pairs[:, 2 * th + tl, PAIRS * gl + u : PAIRS * (gl + 1) : 2],
                                     ident[:],
                                 )
-                        banks.append(tp)
+                        banks.append(turned)
                 return banks
 
             def copy_out_run(r, banks):
-                grps = []
+                tiles = []
                 for gl in range(2):
-                    grp = new_grp()
-                    gw = grp[:].bitcast(F32)
-                    for ah in range(2):
+                    grouped = new_grouped()
+                    pairs = grouped[:].bitcast(F32)
+                    for th in range(2):
                         nc.scalar.copy(
-                            out=gw[:, 256 * ah : 256 * (ah + 1), :].rearrange("p (a r) u -> p a r u", a=2),
-                            in_=banks[2 * gl + ah][:].rearrange("p a u r -> p a r u"),
+                            out=pairs[:, 2 * P * th : 2 * P * (th + 1), :].rearrange("p (tl r) u -> p tl r u", tl=2),
+                            in_=banks[2 * gl + th][:].rearrange("p tl u r -> p tl r u"),
                         )
-                    grps.append(grp)
-                tgrps[r] = grps
+                    tiles.append(grouped)
+                run_grouped[r] = tiles
 
             def quantize_run(r):
-                if r < N_W_RUNS:
+                if r < W_RUNS:
                     a, h = divmod(r, 2)
-                    codes, planes = w_codes[a], w_planes[a]
+                    codes, scales = w_codes[a], w_scales[a]
                 else:
-                    a, h = divmod(r - N_W_RUNS, 2)
-                    codes, planes = k_codes[a], k_planes[a]
+                    a, h = divmod(r - W_RUNS, 2)
+                    codes, scales = k_codes[a], k_scales[a]
                 for gl in range(2):
-                    quantize(tgrps[r][gl], codes, planes, 2 * h + gl)
+                    quantize(run_grouped[r][gl], codes, scales, 2 * h + gl)
 
-            def project_half(u, hf):
-                b, a = divmod(u, 4)
+            def project_half(u, half):
+                b, a = divmod(u, PASSES)
                 banks = []
-                for t in (2 * hf, 2 * hf + 1):
-                    banks.append(mx_bank(w_codes[a], w_planes[a], slice(P * t, P * (t + 1)), x_codes[b], x_planes[b]))
+                for t in (2 * half, 2 * half + 1):
+                    banks.append(mx_bank(w_codes[a], w_scales[a], slice(P * t, P * (t + 1)), x_codes[b], x_scales[b]))
                 return banks
 
-            def evacuate_half(u, hf, banks):
-                a = u % 4
-                if hf == 0:
-                    qbfs[u] = ph1.tile([P, 4, BANK], BF16, name="qbf", tag="qbf", bufs=2, align_bytes=64)
+            def evacuate_half(u, half, banks):
+                a = u % PASSES
+                if half == 0:
+                    q_bf16[u] = ph1.tile([P, PACK, BANK], BF16, name="qbf", tag="qbf", bufs=NEXT_AND_NOW, align_bytes=64)
                 for i in range(2):
-                    t = 2 * hf + i
+                    t = 2 * half + i
                     nc.scalar.activation(
-                        out=qbfs[u][:, t, :],
+                        out=q_bf16[u][:, t, :],
                         in_=banks[i][:],
                         func=ACT.Identity,
-                        bias=bias[:, 4 * a + t : 4 * a + t + 1],
+                        bias=bias[:, PACK * a + t : PACK * a + t + 1],
                         scale=inv_sqrt_c,
                     )
 
             def interleave_q(u):
-                grp = new_grp()
-                nc.vector.tensor_copy(out=grp[:], in_=qbfs[u][:].rearrange("p t n -> p n t"))
-                qgrps[u] = grp
+                grouped = new_grouped()
+                nc.vector.tensor_copy(out=grouped[:], in_=q_bf16[u][:].rearrange("p t n -> p n t"))
+                q_grouped[u] = grouped
 
             def quantize_q(u):
-                b, a = divmod(u, 4)
+                b, a = divmod(u, PASSES)
                 if a == 0 and b >= len(q_codes):
-                    q_codes.append(rawq.tile([P, PASSES, BANK], U32, name="q_late", tag="rawq", align_bytes=64))
-                quantize(qgrps[u], q_codes[b], q_planes[b], a)
+                    q_codes.append(rawq.tile([P, PASSES, BANK], U32, name="q_late", tag="rawq", align_bytes=256))
+                quantize(q_grouped[u], q_codes[b], q_scales[b], a)
 
-            items = [("R", 0, 0), ("R", 1, 0), ("R", 2, 0)]
-            r_next = 3
-            for u in range(N_UNITS):
-                for hf in range(2):
-                    items.append(("U", u, hf))
-                    if r_next < N_RUNS and (u < 4 or hf == 1):
-                        items.append(("R", r_next, 0))
-                        r_next += 1
+            steps = [("run", r, 0) for r in range(PIECE_BUFS)]
+            next_run = PIECE_BUFS
+            for u in range(UNITS):
+                for half in range(2):
+                    steps.append(("half", u, half))
+                    if next_run < RUNS and (u < UNITS_WITH_TWO_RUNS or half == 1):
+                        steps.append(("run", next_run, 0))
+                        next_run += 1
 
-            for r in range(RAW_BUFS):
-                load_raw(r)
-            for c in range(4):
+            for r in range(PIECE_BUFS):
+                load_piece(r)
+            for c in range(X_BUFS):
                 load_x(c)
-            nc.vector.tensor_scalar(
-                out=bias[:], in0=bq_raw[:].rearrange("p a t -> p (a t)"), scalar1=inv_sqrt_c, scalar2=None, op0=ALU.mult
-            )
+            nc.sync.dma_start(out=bq_raw[:], in_=bq.rearrange("(a p t) -> p a t", a=PASSES, t=PACK))
 
-            pending_q = []
-            prev = None
-            head_x_done = False
-            for item in items:
-                kind, n, hf = item
-                x_chunk = None
-                if kind == "U" and not head_x_done:
-                    for c in range(4):
-                        interleave_x(c, HEAD_X_ON_SCALAR)
+            to_quantize = []
+            last = None
+            for step in steps:
+                kind, n, half = step
+                chunk = None
+                if step == ("half", 0, 0):
+                    for c in range(PASSES):
+                        interleave_x(c, X_ON_SCALAR_BLOCK_0)
                         load_x(c + X_BUFS)
                         if c > 0:
                             quantize_x(c - 1)
-                    if prev is not None and prev[0] == "R":
-                        quantize_run(prev[1])
-                        prev = None
-                    quantize_x(3)
-                    head_x_done = True
-                if kind == "R":
+                    quantize_run(last[1])
+                    last = None
+                    quantize_x(PASSES - 1)
+                    nc.vector.tensor_scalar(
+                        out=bias[:],
+                        in0=bq_raw[:].rearrange("p a t -> p (a t)"),
+                        scalar1=inv_sqrt_c,
+                        scalar2=None,
+                        op0=ALU.mult,
+                    )
+                if kind == "run":
                     banks = transpose_run(n)
-                    if n + RAW_BUFS < N_RUNS:
-                        load_raw(n + RAW_BUFS)
+                    if n + PIECE_BUFS < RUNS:
+                        load_piece(n + PIECE_BUFS)
                 else:
-                    banks = project_half(n, hf)
-                if kind == "U" and hf == 0 and n + 4 < N_UNITS:
-                    x_chunk = n + 4
-                    interleave_x(x_chunk, LATE_X_ON_SCALAR if n >= FIRST_UNIT_WITHOUT_RUN else 0)
-                    if x_chunk + X_BUFS < N_UNITS:
-                        load_x(x_chunk + X_BUFS)
-                if kind == "R":
+                    banks = project_half(n, half)
+                if kind == "half" and half == 0 and n + PASSES < UNITS:
+                    chunk = n + PASSES
+                    interleave_x(chunk, X_ON_SCALAR_LATE if n >= FIRST_UNIT_WITHOUT_RUN else 0)
+                    if chunk + X_BUFS < UNITS:
+                        load_x(chunk + X_BUFS)
+                if kind == "run":
                     copy_out_run(n, banks)
                 else:
-                    evacuate_half(n, hf, banks)
-                for u in pending_q:
+                    evacuate_half(n, half, banks)
+                for u in to_quantize:
                     quantize_q(u)
-                pending_q = []
-                if prev is not None:
-                    if prev[0] == "R":
-                        quantize_run(prev[1])
-                    elif prev[2] == 1:
-                        interleave_q(prev[1])
-                        pending_q.append(prev[1])
-                if x_chunk is not None:
-                    quantize_x(x_chunk)
-                prev = item
-            interleave_q(prev[1])
-            quantize_q(prev[1])
+                to_quantize = []
+                if last is not None:
+                    if last[0] == "run":
+                        quantize_run(last[1])
+                    elif last[2] == 1:
+                        interleave_q(last[1])
+                        to_quantize.append(last[1])
+                if chunk is not None:
+                    quantize_x(chunk)
+                last = step
+            interleave_q(UNITS - 1)
+            quantize_q(UNITS - 1)
 
-        with tc.tile_pool(name="ph2", bufs=4) as ph2:
-            state = {}
+        with tc.tile_pool(name="ph2", bufs=STAT_BUFS) as ph2:
+            rows_of = {}
 
-            def soft_exp(s, e):
-                sc, negmax, tot = state[s]
-                cols = slice(1024 * e, 1024 * (e + 1))
+            def soft_exp(s):
+                row, neg_max = rows_of[s]
+                total = ph2.tile([P, 1], F32, name="tot", tag="tot")
                 nc.scalar.activation(
-                    out=sc[:, cols], in_=sc[:, cols], func=ACT.Exp, bias=negmax[:], scale=-1.0, accum_out=tot[:, e : e + 1]
+                    out=row[:], in_=row[:], func=ACT.Exp, bias=neg_max[:], scale=-1.0, accum_out=total[:]
+                )
+                rows_of[s] = (row, total)
+
+            def on_gpsimd(row, cols, factor):
+                nc.gpsimd.tensor_scalar(
+                    out=row[:, cols], in0=row[:, cols], scalar1=factor[:], scalar2=0.0, op0=ALU.mult, op1=ALU.add
                 )
 
-            def soft_finish(s, last):
-                sc, negmax, tot = state[s]
-                tsum = ph2.tile([P, 1], F32, name="tsum", tag="tsum")
-                nc.vector.tensor_reduce(out=tsum[:], in_=tot[:], axis=AXIS.X, op=ALU.add)
-                rs = ph2.tile([P, 1], F32, name="rs", tag="rs")
-                nc.vector.reciprocal(out=rs[:], in_=tsum[:])
-                rows = slice(P * s, P * (s + 1))
-                if not last:
-                    for h in range(2):
-                        cols = slice(2048 * h, 2048 * (h + 1))
-                        nc.gpsimd.tensor_scalar(
-                            out=sc[:, cols], in0=sc[:, cols], scalar1=rs[:], scalar2=0.0, op0=ALU.mult, op1=ALU.add
-                        )
-                        nc.sync.dma_start(out=out2[rows, cols], in_=sc[:, cols])
-                else:
-                    nc.gpsimd.tensor_scalar(
-                        out=sc[:, 3072:4096], in0=sc[:, 3072:4096], scalar1=rs[:], scalar2=0.0, op0=ALU.mult, op1=ALU.add
-                    )
-                    nc.scalar.activation(out=sc[:, 2048:3072], in_=sc[:, 2048:3072], func=ACT.Copy, scale=rs[:])
-                    for h in range(2):
-                        cols = slice(1024 * h, 1024 * (h + 1))
-                        nc.vector.tensor_scalar(out=sc[:, cols], in0=sc[:, cols], scalar1=rs[:], scalar2=None, op0=ALU.mult)
-                        nc.sync.dma_start(out=out2[rows, cols], in_=sc[:, cols])
-                    nc.sync.dma_start(out=out2[rows, 2048:3072], in_=sc[:, 2048:3072])
-                    nc.sync.dma_start(out=out2[rows, 3072:4096], in_=sc[:, 3072:4096])
+            def store(s, row, cols):
+                nc.sync.dma_start(out=out2[P * s : P * (s + 1), cols], in_=row[:, cols])
 
-            for s in range(N_TILES):
-                b, j = divmod(s, 4)
-                sc = ph2.tile([P, KEYS], F32, name="sc", tag="sc", bufs=SCORE_BUFS)
-                nm = ph2.tile([P, 8], F32, name="nm", tag="nm")
-                for kb in range(8):
-                    cols = slice(BANK * kb, BANK * (kb + 1))
-                    if s > 0 and kb % 2 == 0:
-                        soft_exp(s - 1, kb // 2)
-                    acc = mx_bank(q_codes[b], q_planes[b], slice(P * j, P * (j + 1)), k_codes[kb], k_planes[kb])
-                    if kb % 2 == 0:
-                        nc.scalar.activation(out=sc[:, cols], in_=acc[:], func=ACT.Copy, scale=-1.0)
-                    else:
-                        if kb == 7:
-                            if s > 0:
-                                soft_finish(s - 1, False)
-                            nc.vector.tensor_reduce(
-                                out=nm[:, 6:7], in_=sc[:, BANK * 6 : BANK * 7], axis=AXIS.X, op=ALU.min
-                            )
-                        nc.vector.tensor_scalar(
-                            out=sc[:, cols],
-                            in0=acc[:],
-                            scalar1=-1.0,
-                            scalar2=None,
-                            op0=ALU.mult,
-                            op1=ALU.min,
-                            accum_out=nm[:, kb : kb + 1],
-                        )
-                        if kb < 7:
-                            nc.vector.tensor_reduce(
-                                out=nm[:, kb - 1 : kb], in_=sc[:, BANK * (kb - 1) : BANK * kb], axis=AXIS.X, op=ALU.min
-                            )
-                negmax = ph2.tile([P, 1], F32, name="negmax", tag="negmax")
-                nc.vector.tensor_reduce(out=negmax[:], in_=nm[:], axis=AXIS.X, op=ALU.min)
-                tot = ph2.tile([P, EXP_PIECES], F32, name="tot", tag="tot")
-                state[s] = (sc, negmax, tot)
-            for e in range(EXP_PIECES):
-                soft_exp(N_TILES - 1, e)
-            soft_finish(N_TILES - 1, True)
+            def soft_finish(s):
+                row, total = rows_of[s]
+                factor = ph2.tile([P, 1], F32, name="rs", tag="rs")
+                nc.vector.reciprocal(out=factor[:], in_=total[:])
+                for h in range(2):
+                    cols = slice(KEYS // 2 * h, KEYS // 2 * (h + 1))
+                    on_gpsimd(row, cols, factor)
+                    store(s, row, cols)
+
+            def soft_finish_last(s):
+                row, total = rows_of[s]
+                factor = ph2.tile([P, 1], F32, name="rs", tag="rs")
+                nc.vector.reciprocal(out=factor[:], in_=total[:])
+                quarter = [slice(KEYS // 4 * i, KEYS // 4 * (i + 1)) for i in range(4)]
+                on_gpsimd(row, quarter[3], factor)
+                nc.scalar.activation(out=row[:, quarter[2]], in_=row[:, quarter[2]], func=ACT.Copy, scale=factor[:])
+                for i in range(2):
+                    nc.vector.tensor_scalar(
+                        out=row[:, quarter[i]], in0=row[:, quarter[i]], scalar1=factor[:], scalar2=None, op0=ALU.mult
+                    )
+                    store(s, row, quarter[i])
+                store(s, row, quarter[2])
+                store(s, row, quarter[3])
+
+            for s in range(TILES):
+                b, j = divmod(s, ROW_GROUPS)
+                if s > 0:
+                    soft_exp(s - 1)
+                row = ph2.tile([P, KEYS], F32, name="sc", tag="sc", bufs=SCORE_BUFS)
+                neg_max_of_bank = ph2.tile([P, KEY_BANKS], F32, name="nm", tag="nm")
+                for kb in range(KEY_BANKS):
+                    acc = mx_bank(q_codes[b], q_scales[b], slice(P * j, P * (j + 1)), k_codes[kb], k_scales[kb])
+                    nc.vector.tensor_scalar(
+                        out=row[:, BANK * kb : BANK * (kb + 1)],
+                        in0=acc[:],
+                        scalar1=-1.0,
+                        scalar2=None,
+                        op0=ALU.mult,
+                        op1=ALU.min,
+                        accum_out=neg_max_of_bank[:, kb : kb + 1],
+                    )
+                    if kb == FINISH_AFTER_BANK and s > 0:
+                        soft_finish(s - 1)
+                neg_max = ph2.tile([P, 1], F32, name="negmax", tag="negmax")
+                nc.vector.tensor_reduce(out=neg_max[:], in_=neg_max_of_bank[:], axis=AXIS.X, op=ALU.min)
+                rows_of[s] = (row, neg_max)
+            soft_exp(TILES - 1)
+            soft_finish_last(TILES - 1)

@@ -74,13 +74,13 @@ def tile_visionattention_pa_l_kernel(tc, x, Wq, bq, k, out):
         bias = keep.tile([P, PASSES * PACK], F32, name="bias")
 
         k_codes = []
-        k_scales = []
         q_codes = []
-        q_scales = []
+        k_scales_all = keep.tile([P, KEY_BANKS, BANK], U8, name="k_planes", align_bytes=256)
+        q_scales_all = keep.tile([P, BLOCKS, BANK], U8, name="q_planes", align_bytes=256)
+        k_scales = [k_scales_all[:, i, :] for i in range(KEY_BANKS)]
+        q_scales = [q_scales_all[:, i, :] for i in range(BLOCKS)]
         for i in range(KEY_BANKS):
             k_codes.append(keep.tile([P, PASSES, BANK], U32, name="k_codes%d" % i, align_bytes=256))
-            k_scales.append(keep.tile([P, BANK], U8, name="k_planes%d" % i, align_bytes=64))
-            q_scales.append(keep.tile([P, BANK], U8, name="q_planes%d" % i, align_bytes=64))
         for i in range(BLOCKS - PIECE_BUFS):
             q_codes.append(keep.tile([P, PASSES, BANK], U32, name="q_codes%d" % i, align_bytes=256))
 
@@ -107,10 +107,10 @@ def tile_visionattention_pa_l_kernel(tc, x, Wq, bq, k, out):
 
         with tc.tile_pool(name="ph1", bufs=1) as ph1:
             w_codes = []
-            w_scales = []
+            w_scales_all = ph1.tile([P, PASSES, BANK], U8, name="w_planes", align_bytes=256)
+            w_scales = [w_scales_all[:, i, :] for i in range(PASSES)]
             for i in range(PASSES):
                 w_codes.append(ph1.tile([P, PASSES, BANK], U32, name="w_codes%d" % i, align_bytes=256))
-                w_scales.append(ph1.tile([P, BANK], U8, name="w_planes%d" % i, align_bytes=64))
 
             pieces = {}
             run_grouped = {}
@@ -158,7 +158,7 @@ def tile_visionattention_pa_l_kernel(tc, x, Wq, bq, k, out):
                 b, g = divmod(c, PASSES)
                 if g == 0:
                     x_codes[b] = ph1.tile([P, PASSES, BANK], U32, name="xc", tag="xc", bufs=NEXT_AND_NOW, align_bytes=256)
-                    x_scales[b] = ph1.tile([P, BANK], U8, name="xp", tag="xp", bufs=NEXT_AND_NOW, align_bytes=64)
+                    x_scales[b] = ph1.tile([P, BANK], U8, name="xp", tag="xp", bufs=NEXT_AND_NOW, align_bytes=256)
                 quantize(x_grouped[c], x_codes[b], x_scales[b], g)
 
             def transpose_run(r):

import math
from contextlib import ExitStack

import concourse.masks as masks
import concourse.mybir as mybir

F32 = mybir.dt.float32
BF16 = mybir.dt.bfloat16
U32 = mybir.dt.uint32
U8 = mybir.dt.uint8
FP8X4 = mybir.dt.float8_e4m3fn_x4
ALU = mybir.AluOpType
ACT = mybir.ActivationFunctionType
AXIS = mybir.AxisListType

P = 128
C = 2048
TOKENS = 4096
KEYS = 4096
PACK = 4
PASSES = C // (P * PACK)
BANK = 512
PSUM_BANKS = 8
ROW_GROUPS = BANK // P
PAIRS = P * PACK // 2

BLOCKS = TOKENS // BANK
UNITS = BLOCKS * (C // BANK)
TILES = TOKENS // P
KEY_BANKS = KEYS // BANK

PIECE = 1024
W_RUNS = (C // BANK) * (C // PIECE)
RUNS = W_RUNS + (KEYS // BANK) * (C // PIECE)
UNITS_WITH_TWO_RUNS = 4
FIRST_UNIT_WITHOUT_RUN = 17

PIECE_BUFS = 3
X_BUFS = 4
GROUPED_BUFS = 5
SCORE_BUFS = 6
NEXT_AND_NOW = 2
STAT_BUFS = 4

X_ON_SCALAR_BLOCK_0 = 192
X_ON_SCALAR_LATE = 256

FINISH_AFTER_BANK = 4

FLOPS = 2 * TOKENS * C * C + 2 * TOKENS * KEYS * C


def tile_visionattention_pa_l_kernel(tc, x, Wq, bq, k, out):
    nc = tc.nc
    inv_sqrt_c = 1.0 / math.sqrt(C)
    x2 = x.rearrange("b c h w -> (b c) (h w)")
    k2 = k.rearrange("b m c -> (b m) c")
    out2 = out.rearrange("b n m -> (b n) m")

    with ExitStack() as ctx:
        keep = ctx.enter_context(tc.tile_pool(name="keep", bufs=1))
        rawq = ctx.enter_context(tc.tile_pool(name="rawq", bufs=PIECE_BUFS))
        psum = ctx.enter_context(tc.psum_pool(name="psum", bufs=PSUM_BANKS))

        ident = keep.tile([P, P], F32, name="ident")
        masks.make_identity(nc, ident[:])

        ctx.enter_context(tc.manual_schedule())

        bq_raw = keep.tile([P, PASSES, PACK], BF16, name="bq_raw")
        warm = keep.tile([P, 1], F32, name="warm")
        nc.vector.memset(warm[:], 0.0)
        nc.scalar.activation(out=warm[:], in_=warm[:], func=ACT.Exp)
        bias = keep.tile([P, PASSES * PACK], F32, name="bias")

        k_codes = []
        q_codes = []
        k_scales_all = keep.tile([P, KEY_BANKS, BANK], U8, name="k_planes", align_bytes=256)
        q_scales_all = keep.tile([P, BLOCKS, BANK], U8, name="q_planes", align_bytes=256)
        k_scales = [k_scales_all[:, i, :] for i in range(KEY_BANKS)]
        q_scales = [q_scales_all[:, i, :] for i in range(BLOCKS)]
        for i in range(KEY_BANKS):
            k_codes.append(keep.tile([P, PASSES, BANK], U32, name="k_codes%d" % i, align_bytes=256))
        for i in range(BLOCKS - PIECE_BUFS):
            q_codes.append(keep.tile([P, PASSES, BANK], U32, name="q_codes%d" % i, align_bytes=256))

        def quantize(grouped, codes, scales, g):
            nc.vector.quantize_mx(
                out=codes[:, g, :].bitcast(FP8X4),
                scales=scales[4 * g : P, :],
                in_=grouped[:].rearrange("p n j -> p (n j)"),
            )

        def mx_bank(stat_codes, stat_scales, cols, mov_codes, mov_scales):
            acc = psum.tile([P, BANK], F32, name="acc", tag="bank")
            for g in range(PASSES):
                nc.tensor.matmul_mx(
                    out=acc[:],
                    lhsT=stat_codes[:, g, cols].bitcast(FP8X4),
                    lhsT_scale=stat_scales[4 * g : P, cols],
                    rhs=mov_codes[:, g, :].bitcast(FP8X4),
                    rhs_scale=mov_scales[4 * g : P, :],
                    start=(g == 0),
                    stop=(g == PASSES - 1),
                )
            return acc

        with tc.tile_pool(name="ph1", bufs=1) as ph1:
            w_codes = []
            w_scales_all = ph1.tile([P, PASSES, BANK], U8, name="w_planes", align_bytes=256)
            w_scales = [w_scales_all[:, i, :] for i in range(PASSES)]
            for i in range(PASSES):
                w_codes.append(ph1.tile([P, PASSES, BANK], U32, name="w_codes%d" % i, align_bytes=256))

            pieces = {}
            run_grouped = {}
            x_loaded = {}
            x_grouped = {}
            x_codes = {}
            x_scales = {}
            q_bf16 = {}
            q_grouped = {}

            def load_piece(r):
                piece = rawq.tile([P, ROW_GROUPS, PIECE], BF16, name="raw", tag="rawq", align_bytes=256)
                if r < W_RUNS:
                    a, h = divmod(r, 2)
                    source = Wq[BANK * a : BANK * (a + 1), PIECE * h : PIECE * (h + 1)].rearrange(
                        "(m t) c -> m t c", t=ROW_GROUPS
                    )
                else:
                    a, h = divmod(r - W_RUNS, 2)
                    source = k2[BANK * a : BANK * (a + 1), PIECE * h : PIECE * (h + 1)].rearrange("(t p) c -> p t c", p=P)
                nc.sync.dma_start(out=piece[:], in_=source)
                pieces[r] = piece

            def load_x(c):
                b, g = divmod(c, PASSES)
                loaded = ph1.tile([P, PACK, BANK], BF16, name="xr", tag="xr", bufs=X_BUFS, align_bytes=64)
                source = x2[BANK * g : BANK * (g + 1), BANK * b : BANK * (b + 1)].rearrange("(p j) n -> p j n", j=PACK)
                nc.sync.dma_start(out=loaded[:], in_=source)
                x_loaded[c] = loaded

            def new_grouped():
                grouped = ph1.tile([P, BANK, PACK], BF16, name="grp", tag="grp", bufs=GROUPED_BUFS, align_bytes=64)
                return grouped

            def interleave_x(c, on_scalar):
                grouped = new_grouped()
                loaded = x_loaded[c]
                cut = BANK - on_scalar
                nc.vector.tensor_copy(out=grouped[:, 0:cut, :], in_=loaded[:, :, 0:cut].rearrange("p j n -> p n j"))
                if on_scalar > 0:
                    nc.scalar.copy(out=grouped[:, cut:BANK, :], in_=loaded[:, :, cut:BANK].rearrange("p j n -> p n j"))
                x_grouped[c] = grouped

            def quantize_x(c):
                b, g = divmod(c, PASSES)
                if g == 0:
                    x_codes[b] = ph1.tile([P, PASSES, BANK], U32, name="xc", tag="xc", bufs=NEXT_AND_NOW, align_bytes=256)
                    x_scales[b] = ph1.tile([P, BANK], U8, name="xp", tag="xp", bufs=NEXT_AND_NOW, align_bytes=256)
                quantize(x_grouped[c], x_codes[b], x_scales[b], g)

            def transpose_run(r):
                pairs = pieces[r][:].bitcast(F32)
                banks = []
                for gl in range(2):
                    for th in range(2):
                        turned = psum.tile([P, 2, 2, P], F32, name="tp", tag="bank")
                        for tl in range(2):
                            for u in range(2):
                                nc.tensor.transpose(
                                    turned[:, tl, u, :],
                                    pairs[:, 2 * th + tl, PAIRS * gl + u : PAIRS * (gl + 1) : 2],
                                    ident[:],
                                )
                        banks.append(turned)
                return banks

            def copy_out_run(r, banks):
                tiles = []
                for gl in range(2):
                    grouped = new_grouped()
                    pairs = grouped[:].bitcast(F32)
                    for th in range(2):
                        nc.scalar.copy(
                            out=pairs[:, 2 * P * th : 2 * P * (th + 1), :].rearrange("p (tl r) u -> p tl r u", tl=2),
                            in_=banks[2 * gl + th][:].rearrange("p tl u r -> p tl r u"),
                        )
                    tiles.append(grouped)
                run_grouped[r] = tiles

            def quantize_run(r):
                if r < W_RUNS:
                    a, h = divmod(r, 2)
                    codes, scales = w_codes[a], w_scales[a]
                else:
                    a, h = divmod(r - W_RUNS, 2)
                    codes, scales = k_codes[a], k_scales[a]
                for gl in range(2):
                    quantize(run_grouped[r][gl], codes, scales, 2 * h + gl)

            def project_half(u, half):
                b, a = divmod(u, PASSES)
                banks = []
                for t in (2 * half, 2 * half + 1):
                    banks.append(mx_bank(w_codes[a], w_scales[a], slice(P * t, P * (t + 1)), x_codes[b], x_scales[b]))
                return banks

            def evacuate_half(u, half, banks):
                a = u % PASSES
                if half == 0:
                    q_bf16[u] = ph1.tile([P, PACK, BANK], BF16, name="qbf", tag="qbf", bufs=NEXT_AND_NOW, align_bytes=64)
                for i in range(2):
                    t = 2 * half + i
                    nc.scalar.activation(
                        out=q_bf16[u][:, t, :],
                        in_=banks[i][:],
                        func=ACT.Identity,
                        bias=bias[:, PACK * a + t : PACK * a + t + 1],
                        scale=inv_sqrt_c,
                    )

            def interleave_q(u):
                grouped = new_grouped()
                nc.vector.tensor_copy(out=grouped[:], in_=q_bf16[u][:].rearrange("p t n -> p n t"))
                q_grouped[u] = grouped

            def quantize_q(u):
                b, a = divmod(u, PASSES)
                if a == 0 and b >= len(q_codes):
                    q_codes.append(rawq.tile([P, PASSES, BANK], U32, name="q_late", tag="rawq", align_bytes=256))
                quantize(q_grouped[u], q_codes[b], q_scales[b], a)

            steps = [("run", r, 0) for r in range(PIECE_BUFS)]
            next_run = PIECE_BUFS
            for u in range(UNITS):
                for half in range(2):
                    steps.append(("half", u, half))
                    if next_run < RUNS and (u < UNITS_WITH_TWO_RUNS or half == 1):
                        steps.append(("run", next_run, 0))
                        next_run += 1

            for r in range(PIECE_BUFS):
                load_piece(r)
            for c in range(X_BUFS):
                load_x(c)
            nc.sync.dma_start(out=bq_raw[:], in_=bq.rearrange("(a p t) -> p a t", a=PASSES, t=PACK))

            to_quantize = []
            last = None
            for step in steps:
                kind, n, half = step
                chunk = None
                if step == ("half", 0, 0):
                    for c in range(PASSES):
                        interleave_x(c, X_ON_SCALAR_BLOCK_0)
                        load_x(c + X_BUFS)
                        if c > 0:
                            quantize_x(c - 1)
                    quantize_run(last[1])
                    last = None
                    quantize_x(PASSES - 1)
                    nc.vector.tensor_scalar(
                        out=bias[:],
                        in0=bq_raw[:].rearrange("p a t -> p (a t)"),
                        scalar1=inv_sqrt_c,
                        scalar2=None,
                        op0=ALU.mult,
                    )
                if kind == "run":
                    banks = transpose_run(n)
                    if n + PIECE_BUFS < RUNS:
                        load_piece(n + PIECE_BUFS)
                else:
                    banks = project_half(n, half)
                if kind == "half" and half == 0 and n + PASSES < UNITS:
                    chunk = n + PASSES
                    interleave_x(chunk, X_ON_SCALAR_LATE if n >= FIRST_UNIT_WITHOUT_RUN else 0)
                    if chunk + X_BUFS < UNITS:
                        load_x(chunk + X_BUFS)
                if kind == "run":
                    copy_out_run(n, banks)
                else:
                    evacuate_half(n, half, banks)
                for u in to_quantize:
                    quantize_q(u)
                to_quantize = []
                if last is not None:
                    if last[0] == "run":
                        quantize_run(last[1])
                    elif last[2] == 1:
                        interleave_q(last[1])
                        to_quantize.append(last[1])
                if chunk is not None:
                    quantize_x(chunk)
                last = step
            interleave_q(UNITS - 1)
            quantize_q(UNITS - 1)

        with tc.tile_pool(name="ph2", bufs=STAT_BUFS) as ph2:
            rows_of = {}

            def soft_exp(s):
                row, neg_max = rows_of[s]
                total = ph2.tile([P, 1], F32, name="tot", tag="tot")
                nc.scalar.activation(
                    out=row[:], in_=row[:], func=ACT.Exp, bias=neg_max[:], scale=-1.0, accum_out=total[:]
                )
                rows_of[s] = (row, total)

            def on_gpsimd(row, cols, factor):
                nc.gpsimd.tensor_scalar(
                    out=row[:, cols], in0=row[:, cols], scalar1=factor[:], scalar2=0.0, op0=ALU.mult, op1=ALU.add
                )

            def store(s, row, cols):
                nc.sync.dma_start(out=out2[P * s : P * (s + 1), cols], in_=row[:, cols])

            def soft_finish(s):
                row, total = rows_of[s]
                factor = ph2.tile([P, 1], F32, name="rs", tag="rs")
                nc.vector.reciprocal(out=factor[:], in_=total[:])
                for h in range(2):
                    cols = slice(KEYS // 2 * h, KEYS // 2 * (h + 1))
                    on_gpsimd(row, cols, factor)
                    store(s, row, cols)

            def soft_finish_last(s):
                row, total = rows_of[s]
                factor = ph2.tile([P, 1], F32, name="rs", tag="rs")
                nc.vector.reciprocal(out=factor[:], in_=total[:])
                quarter = [slice(KEYS // 4 * i, KEYS // 4 * (i + 1)) for i in range(4)]
                on_gpsimd(row, quarter[3], factor)
                nc.scalar.activation(out=row[:, quarter[2]], in_=row[:, quarter[2]], func=ACT.Copy, scale=factor[:])
                for i in range(2):
                    nc.vector.tensor_scalar(
                        out=row[:, quarter[i]], in0=row[:, quarter[i]], scalar1=factor[:], scalar2=None, op0=ALU.mult
                    )
                    store(s, row, quarter[i])
                store(s, row, quarter[2])
                store(s, row, quarter[3])

            for s in range(TILES):
                b, j = divmod(s, ROW_GROUPS)
                if s > 0:
                    soft_exp(s - 1)
                row = ph2.tile([P, KEYS], F32, name="sc", tag="sc", bufs=SCORE_BUFS)
                neg_max_of_bank = ph2.tile([P, KEY_BANKS], F32, name="nm", tag="nm")
                for kb in range(KEY_BANKS):
                    acc = mx_bank(q_codes[b], q_scales[b], slice(P * j, P * (j + 1)), k_codes[kb], k_scales[kb])
                    nc.vector.tensor_scalar(
                        out=row[:, BANK * kb : BANK * (kb + 1)],
                        in0=acc[:],
                        scalar1=-1.0,
                        scalar2=None,
                        op0=ALU.mult,
                        op1=ALU.min,
                        accum_out=neg_max_of_bank[:, kb : kb + 1],
                    )
                    if kb == FINISH_AFTER_BANK and s > 0:
                        soft_finish(s - 1)
                neg_max = ph2.tile([P, 1], F32, name="negmax", tag="negmax")
                nc.vector.tensor_reduce(out=neg_max[:], in_=neg_max_of_bank[:], axis=AXIS.X, op=ALU.min)
                rows_of[s] = (row, neg_max)
            soft_exp(TILES - 1)
            soft_finish_last(TILES - 1)
